import numpy as np
import ml_dtypes


def mxq(x, axis, fmt="e4m3"):
    dtype, down = {"e4m3": (ml_dtypes.float8_e4m3fn, 7), "e5m2": (ml_dtypes.float8_e5m2, 14)}[fmt]
    v = np.moveaxis(np.asarray(x, np.float32).astype(ml_dtypes.bfloat16).astype(np.float64), axis, -1)
    blocks = v.reshape(v.shape[:-1] + (-1, 32))
    amax = np.abs(blocks).max(-1, keepdims=True)
    byte = np.maximum(np.where(amax > 0, np.frexp(amax)[1] - 1 + 127, 0) - down, 1)
    scale = np.exp2(byte - 127.0)
    codes = (blocks / scale).astype(np.float32).astype(dtype).astype(np.float64)
    return np.moveaxis((codes * scale).reshape(v.shape), -1, axis)


WIDE = False


def mx_kscale(k):
    if not WIDE:
        return np.ones(k)
    levels = np.array([10, -10, 5, -5, 0])
    if k % 512:
        return np.exp2(np.random.permutation(np.resize(levels, k // 32))).repeat(32)
    a = np.empty((k // 512, 16))
    for p in range(k // 512):
        a[p, :8] = np.random.permutation(np.resize(levels, 8))
        for g in range(8):
            far = levels[np.abs(levels - a[p, g]) >= 10]
            a[p, g + 8] = far[np.random.randint(len(far))]
    return np.exp2(a.ravel()).repeat(32)


BF16 = ml_dtypes.bfloat16


def bf(x):
    return np.asarray(x, np.float32).astype(BF16)


def f64(x):
    return np.asarray(x).astype(np.float64)


N, D, H = 1024, 2048, 1024
H2 = H + H
LN_EPS = 1e-5
ERF_TERMS = 120


def erf(x):
    a = np.clip(x, -6.0, 6.0)
    term = a
    total = a
    for n in range(1, ERF_TERMS):
        term = term * (2.0 * a * a / (2.0 * n + 1.0))
        total = total + term
    return 2.0 / np.sqrt(np.pi) * np.exp(-a * a) * total


def gelu(v):
    return 0.5 * v * (1.0 + erf(v / np.sqrt(2.0)))


def layernorm(x, g, b):
    m = x.mean(-1, keepdims=True)
    v = np.square(x - m).mean(-1, keepdims=True)
    return (x - m) / np.sqrt(v + LN_EPS) * g + b


def setup_inputs():
    s, t = mx_kscale(D), mx_kscale(H2)
    return {
        "z": bf(np.random.standard_normal((N, D)) * s),
        "attention_out": bf(np.random.standard_normal((N, H)) * t[H:]),
        "Wz": bf(np.random.standard_normal((H, D)) / np.sqrt(D) / s),
        "bz": bf(0.1 * np.random.standard_normal(H)),
        "gz": bf((1.0 + 0.1 * np.random.standard_normal(H)) * t[:H]),
        "bz_ln": bf(0.1 * np.random.standard_normal(H) * t[:H]),
        "w1_deq": bf(np.random.standard_normal((H, H2)) / np.sqrt(H2) / t),
        "b1": bf(0.1 * np.random.standard_normal(H)),
        "g1": bf(1.0 + 0.1 * np.random.standard_normal(H)),
        "b1_ln": bf(0.1 * np.random.standard_normal(H)),
    }


def reference(z, attention_out, Wz, bz, gz, bz_ln, w1_deq, b1, g1, b1_ln):
    z_proj = layernorm((mxq(f64(z), 1, "e4m3") @ mxq(f64(Wz), 1, "e4m3").T) + f64(bz), f64(gz), f64(bz_ln))
    combined = np.concatenate([z_proj, f64(attention_out)], axis=-1)
    y = (mxq(combined, 1, "e4m3") @ mxq(f64(w1_deq), 1, "e4m3").T) + f64(b1)
    return gelu(layernorm(y, f64(g1), f64(b1_ln)))

@@ -1,0 +1,348 @@
+from contextlib import ExitStack
+
+import concourse.mybir as mybir
+from concourse.masks import make_identity
+
+F32 = mybir.dt.float32
+BF16 = mybir.dt.bfloat16
+U32 = mybir.dt.uint32
+U8 = mybir.dt.uint8
+I32 = mybir.dt.int32
+FP8X4 = mybir.dt.float8_e4m3fn_x4
+ALU = mybir.AluOpType
+ACT = mybir.ActivationFunctionType
+
+P = 128
+N_TOK = 1024
+D_IN = 2048
+H = 1024
+BANK = 512
+PASSES = D_IN // 512
+TILES = N_TOK // P
+LN_EPS = 1e-5
+FLOPS = 2 * N_TOK * D_IN * H + 2 * N_TOK * D_IN * H
+
+AHEAD_Z = 5
+AHEAD_M1 = 4
+AHEAD_A = 3
+AHEAD_ROWS = 2
+DRAIN_ROUNDS = 2
+
+
+def tile_synapsemodel_pa_kernel(tc, z, attention_out, Wz, bz, gz, bz_ln, w1_deq, b1, g1, b1_ln, out):
+    nc = tc.nc
+    with ExitStack() as ctx:
+        const = ctx.enter_context(tc.tile_pool(name="const", bufs=1))
+        keep = ctx.enter_context(tc.tile_pool(name="keep", bufs=1))
+        raw = ctx.enter_context(tc.tile_pool(name="raw", bufs=6))
+        rawa = ctx.enter_context(tc.tile_pool(name="rawa", bufs=4))
+        stage = ctx.enter_context(tc.tile_pool(name="stage", bufs=3))
+        stagew = ctx.enter_context(tc.tile_pool(name="stagew", bufs=2))
+        rows1 = ctx.enter_context(tc.tile_pool(name="rows1", bufs=4))
+        rows2 = ctx.enter_context(tc.tile_pool(name="rows2", bufs=2))
+        rows3 = ctx.enter_context(tc.tile_pool(name="rows3", bufs=3))
+        junkp = ctx.enter_context(tc.tile_pool(name="junkp", bufs=1))
+        plan = ctx.enter_context(tc.tile_pool(name="plan", bufs=2))
+        small = ctx.enter_context(tc.tile_pool(name="small", bufs=8))
+        ps_t = ctx.enter_context(tc.psum_pool(name="ps_t", bufs=5))
+        ps_a = ctx.enter_context(tc.psum_pool(name="ps_a", bufs=3))
+        ctx.enter_context(tc.manual_schedule())
+
+        ident = const.tile([P, P], F32, name="ident")
+        make_identity(nc, ident[:])
+        identb = const.tile([P, P], BF16, name="identb")
+        nc.vector.tensor_copy(out=identb[:], in_=ident[:])
+        mhalf = const.tile([P, 1], F32, name="mhalf")
+        nc.vector.memset(mhalf[:], -0.5)
+        eps = const.tile([P, 1], F32, name="eps")
+        nc.vector.memset(eps[:], LN_EPS)
+        vrows1 = const.tile([P, BANK], BF16, name="vrows1")
+        nc.vector.memset(vrows1[:].bitcast(I32), 0)
+        grows = const.tile([P, BANK], BF16, name="grows")
+        nc.vector.memset(grows[:].bitcast(I32), 0)
+        vrows2 = const.tile([P, BANK], BF16, name="vrows2")
+        nc.vector.memset(vrows2[:].bitcast(I32), 0)
+        nc.sync.dma_start(out=vrows1[0:2, :], in_=bz.rearrange("(a c) -> a c", a=2))
+        nc.sync.dma_start(out=grows[0:2, :], in_=gz.rearrange("(a c) -> a c", a=2))
+        nc.sync.dma_start(out=grows[2:4, :], in_=bz_ln.rearrange("(a c) -> a c", a=2))
+        nc.scalar.dma_start(out=vrows2[2:4, :], in_=b1.rearrange("(a c) -> a c", a=2))
+        nc.scalar.dma_start(out=vrows2[4:6, :], in_=g1.rearrange("(a c) -> a c", a=2))
+        nc.scalar.dma_start(out=vrows2[6:8, :], in_=b1_ln.rearrange("(a c) -> a c", a=2))
+
+        zq = keep.tile([P, TILES * 512], U32, name="zq", align_bytes=64)
+        zs = keep.tile([P, TILES * 512], U8, name="zs", align_bytes=64)
+        wq = keep.tile([P, PASSES * H], U32, name="wq", align_bytes=64)
+        ws = keep.tile([P, PASSES * H], U8, name="ws", align_bytes=64)
+        vq = keep.tile([P, PASSES * H], U32, name="vq", align_bytes=64)
+        vs = keep.tile([P, PASSES * H], U8, name="vs", align_bytes=64)
+        pq = keep.tile([P, TILES * 256], U32, name="pq", align_bytes=64)
+        pscl = keep.tile([P, TILES * 256], U8, name="pscl", align_bytes=64)
+        aq = keep.tile([P, TILES * 256], U32, name="aq", align_bytes=64)
+        ascl = keep.tile([P, TILES * 256], U8, name="ascl", align_bytes=64)
+        bc = const.tile([P, 4 * H], BF16, name="bc")
+        gb = const.tile([P, 16], F32, name="gb")
+        wz_rows = Wz.rearrange("(a q t) k -> a t q k", q=P, t=4)
+
+        live = {}
+
+        def load(kind, idx):
+            if kind == "a":
+                t = rawa.tile([P, H], BF16, tag="rawa")
+                src = attention_out[idx * P:(idx + 1) * P, :]
+            else:
+                t = raw.tile([P, D_IN], BF16, tag="raw")
+                if kind == "W":
+                    src = wz_rows[idx // 4, idx % 4]
+                elif kind == "z":
+                    src = z[idx * P:(idx + 1) * P, :]
+                else:
+                    src = w1_deq[idx * P:(idx + 1) * P, :]
+            nc.sync.dma_start(out=t[:], in_=src)
+            live[("raw", kind, idx)] = t
+
+        def spread_row(r):
+            pb = ps_t.tile([P, BANK], F32, tag="tp")
+            nc.tensor.matmul(
+                pb[:], lhsT=identb[:, r:r + 1].to_broadcast([P, P]), rhs=(vrows1 if r < 2 else vrows2)[:],
+                start=True, stop=True,
+            )
+            dst = bc[:, r * BANK:(r + 1) * BANK]
+            if r < 2:
+                nc.vector.tensor_copy(
+                    out=dst.rearrange("p (t q) -> p t q", t=4),
+                    in_=pb[:].rearrange("p (q t) -> p t q", t=4),
+                )
+            else:
+                nc.vector.tensor_copy(out=dst, in_=pb[:])
+
+        def gain_columns():
+            g32 = const.tile([P, BANK], F32, name="g32")
+            nc.vector.tensor_copy(
+                out=g32[:].rearrange("p (t q) -> p t q", t=4), in_=grows[:].rearrange("p (q t) -> p t q", t=4)
+            )
+            pg = ps_t.tile([P, BANK], F32, tag="tp")
+            for t in range(4):
+                nc.tensor.transpose(pg[:, t * P:(t + 1) * P], g32[:, t * P:(t + 1) * P], ident[:])
+            nc.vector.tensor_copy(
+                out=gb[:].rearrange("p (w a t) -> p w a t", w=2, t=4),
+                in_=pg[:].rearrange("p (t r) -> p t r", t=4)[:, :, 0:4].rearrange("p t (w a) -> p w a t", w=2),
+            )
+
+        def transpose_words(kind, idx, b):
+            if not 0 <= idx < TILES:
+                return
+            words = live[("raw", kind, idx)][:].bitcast(F32)
+            xt = ps_t.tile([P, BANK], F32, tag="tp")
+            for s in range(4):
+                c0 = (2 * b + s // 2) * 256
+                nc.tensor.transpose(xt[:, s * P:(s + 1) * P], words[:, c0 + s % 2:c0 + 256:2], ident[:])
+            src = xt[:].rearrange("p (g u r) -> p g r u", g=2, u=2)
+            if kind in ("W", "w"):
+                key = ("grp", kind, idx // 4)
+                if key not in live:
+                    grouped_w = stagew.tile([P, 4 * D_IN], BF16, tag="grpw", align_bytes=64)
+                    live[key] = grouped_w
+                dst = live[key][:].bitcast(F32).rearrange("p (g j r u) -> p g j r u", g=4, j=4, u=2)[
+                    :, 2 * b:2 * b + 2, idx % 4
+                ]
+                if b == 1:
+                    nc.vector.tensor_copy(out=dst, in_=src)
+                else:
+                    nc.scalar.copy(out=dst, in_=src)
+            else:
+                key = ("grp", kind, idx)
+                if key not in live:
+                    if kind == "a":
+                        grouped = stage.tile([P, H], BF16, tag="grpa", align_bytes=64)
+                    else:
+                        grouped = stage.tile([P, D_IN], BF16, tag="grp", align_bytes=64)
+                    live[key] = grouped
+                dst = live[key][:].bitcast(F32)[:, b * BANK:(b + 1) * BANK].rearrange(
+                    "p (g r u) -> p g r u", g=2, u=2
+                )
+                nc.scalar.copy(out=dst, in_=src)
+
+        def quantise_weights(kind, half):
+            cq, cs = (wq, ws) if kind == "W" else (vq, vs)
+            for g in range(PASSES):
+                sl = slice(g * H + half * BANK, g * H + (half + 1) * BANK)
+                nc.vector.quantize_mx(
+                    out=cq[:, sl].bitcast(FP8X4), scales=cs[:, sl],
+                    in_=live[("grp", kind, half)][:, g * D_IN:(g + 1) * D_IN],
+                )
+
+        def quantise_rows(kind, idx):
+            if not 0 <= idx < TILES:
+                return
+            words = 512 if kind == "z" else 256
+            cq, cs = (zq, zs) if kind == "z" else (aq, ascl)
+            sl = slice(idx * words, (idx + 1) * words)
+            nc.vector.quantize_mx(out=cq[:, sl].bitcast(FP8X4), scales=cs[:, sl], in_=live[("grp", kind, idx)][:])
+
+        def mx_group(stg, i, n):
+            if not 0 <= i < TILES:
+                return
+            acc = ps_a.tile([P, BANK], F32, tag="acc")
+            for g in range(PASSES):
+                if stg == 1:
+                    c0 = i * 512 + g * P
+                    lq, ls, rq, rs = zq, zs, wq, ws
+                else:
+                    c0 = i * 256 + (g % 2) * P
+                    lq, ls = (pq, pscl) if g < 2 else (aq, ascl)
+                    rq, rs = vq, vs
+                sl = slice(c0, c0 + P)
+                sr = slice(g * H + n * BANK, g * H + (n + 1) * BANK)
+                nc.tensor.matmul_mx(
+                    out=acc[:], lhsT=lq[:, sl].bitcast(FP8X4), lhsT_scale=ls[:, sl],
+                    rhs=rq[:, sr].bitcast(FP8X4), rhs_scale=rs[:, sr], start=(g == 0), stop=(g == PASSES - 1),
+                )
+            if n == 0:
+                if stg == 1:
+                    y = rows1.tile([P, H], F32, tag="y1")
+                else:
+                    y = rows2.tile([P, H], F32, tag="y2")
+                sums = small.tile([P, 2], F32, tag="sums")
+                live[("y", stg, i)] = y
+                live[("sums", stg, i)] = sums
+            off = (stg - 1) * H + n * BANK
+            nc.vector.scalar_tensor_tensor(
+                out=live[("y", stg, i)][:, n * BANK:(n + 1) * BANK], in0=acc[:], scalar=1.0,
+                in1=bc[:, off:off + BANK], op0=ALU.mult, op1=ALU.add, accum_out=live[("sums", stg, i)][:, n:n + 1],
+            )
+
+        def stats(stg, i):
+            if not 0 <= i < TILES:
+                return
+            junk2 = small.tile([P, 2], F32, tag="junk2")
+            nmean = small.tile([P, 1], F32, tag="nmean")
+            nc.scalar.activation(
+                out=junk2[:], in_=live[("sums", stg, i)][:], func=ACT.Identity, scale=-1.0 / H, accum_out=nmean[:]
+            )
+            junk = junkp.tile([P, H], BF16, tag="junk")
+            ssq = small.tile([P, 1], F32, tag="ssq")
+            nc.scalar.activation(
+                out=junk[:], in_=live[("y", stg, i)][:], func=ACT.Square, bias=nmean[:], scale=1.0, accum_out=ssq[:]
+            )
+            veps = small.tile([P, 1], F32, tag="veps")
+            nc.scalar.activation(out=veps[:], in_=ssq[:], func=ACT.Identity, scale=1.0 / H, bias=eps[:])
+            live[("nmean", stg, i)] = nmean
+            live[("veps", stg, i)] = veps
+
+        def rstd_of(stg, i):
+            if not 0 <= i < TILES:
+                return
+            rstd = small.tile([P, 1], F32, tag="rstd")
+            nc.gpsimd.tensor_tensor(out=rstd[:], in0=live[("veps", stg, i)][:], in1=mhalf[:], op=ALU.pow)
+            live[("rstd", stg, i)] = rstd
+            if stg == 1:
+                y = live[("y", 1, i)]
+                nc.gpsimd.tensor_scalar(
+                    out=y[:], in0=y[:], scalar1=live[("nmean", 1, i)][:], scalar2=rstd[:], op0=ALU.add, op1=ALU.mult
+                )
+
+        def transpose_rows(i, g):
+            if not 0 <= i < TILES:
+                return
+            tp = ps_t.tile([P, BANK], F32, tag="tp")
+            for t in range(4):
+                j = 4 * g + t
+                nc.tensor.transpose(tp[:, t * P:(t + 1) * P], live[("y", 1, i)][:, j * P:(j + 1) * P], ident[:])
+            if g == 0:
+                planar = plan.tile([P, H], BF16, tag="planar")
+                live[("planar", i)] = planar
+            for t in range(4):
+                j = 4 * g + t
+                nc.scalar.activation(
+                    out=live[("planar", i)][:, j * P:(j + 1) * P], in_=tp[:, t * P:(t + 1) * P], func=ACT.Identity,
+                    scale=gb[:, j:j + 1], bias=gb[:, 8 + j:9 + j],
+                )
+
+        def regroup(i):
+            if not 0 <= i < TILES:
+                return
+            gp = plan.tile([P, H], BF16, tag="gp", align_bytes=64)
+            nc.vector.tensor_copy(
+                out=gp[:].rearrange("p (g c t) -> p g c t", g=2, t=4),
+                in_=live[("planar", i)][:].rearrange("p (g t c) -> p g c t", g=2, t=4),
+            )
+            sl = slice(i * 256, (i + 1) * 256)
+            nc.vector.quantize_mx(out=pq[:, sl].bitcast(FP8X4), scales=pscl[:, sl], in_=gp[:])
+
+        def gain(i):
+            if not 0 <= i < TILES:
+                return
+            t2 = rows3.tile([P, H], F32, tag="t2")
+            nc.vector.scalar_tensor_tensor(
+                out=t2[:], in0=live[("y", 2, i)][:], scalar=live[("nmean", 2, i)][:], in1=bc[:, 2 * H:3 * H],
+                op0=ALU.add, op1=ALU.mult,
+            )
+            live[("t2", i)] = t2
+
+        def shift(i):
+            if not 0 <= i < TILES:
+                return
+            t2 = live[("t2", i)]
+            nc.vector.scalar_tensor_tensor(
+                out=t2[:], in0=t2[:], scalar=live[("rstd", 2, i)][:], in1=bc[:, 3 * H:4 * H], op0=ALU.mult, op1=ALU.add
+            )
+
+        def gelu_store(i):
+            if not 0 <= i < TILES:
+                return
+            t2 = live[("t2", i)]
+            nc.scalar.activation(out=t2[:], in_=t2[:], func=ACT.Gelu)
+            nc.sync.dma_start(out=out[i * P:(i + 1) * P, :], in_=t2[:])
+
+        for j in range(TILES):
+            load("W", j)
+        for r in range(-AHEAD_Z, TILES - AHEAD_A):
+            if r + AHEAD_Z < TILES:
+                load("z", r + AHEAD_Z)
+            for j in (2 * (r + AHEAD_Z), 2 * (r + AHEAD_Z) + 1):
+                if j < TILES:
+                    load("w", j)
+                if j % 2 == 0 and r + AHEAD_A >= 0:
+                    load("a", r + AHEAD_A)
+
+        for j in range(TILES):
+            transpose_words("W", j, 0)
+            transpose_words("W", j, 1)
+            if j == 1:
+                spread_row(0)
+                spread_row(1)
+                gain_columns()
+            if j >= 2:
+                spread_row(j)
+            if j == 4:
+                quantise_weights("W", 0)
+
+        for r in range(-AHEAD_Z, TILES + DRAIN_ROUNDS):
+            w_first = 2 * (r + AHEAD_Z)
+            mx_group(2, r, 0)
+            regroup(r + 1)
+            transpose_words("z", r + AHEAD_Z, 0)
+            rstd_of(2, r - 1)
+            transpose_words("z", r + AHEAD_Z, 1)
+            if w_first == 0:
+                quantise_weights("W", 1)
+            elif w_first in (4, 8):
+                quantise_weights("w", w_first // 4 - 1)
+            transpose_words("w", w_first, 0)
+            transpose_words("w", w_first, 1)
+            mx_group(2, r, 1)
+            stats(1, r + AHEAD_M1 - 1)
+            rstd_of(1, r + AHEAD_M1 - 1)
+            gelu_store(r - 2)
+            transpose_words("a", r + AHEAD_A, 0)
+            mx_group(1, r + AHEAD_M1, 0)
+            transpose_rows(r + AHEAD_ROWS, 0)
+            transpose_words("w", w_first + 1, 0)
+            transpose_words("w", w_first + 1, 1)
+            quantise_rows("z", r + AHEAD_Z)
+            stats(2, r)
+            mx_group(1, r + AHEAD_M1, 1)
+            quantise_rows("a", r + AHEAD_A)
+            shift(r - 1)
+            gain(r)
+            transpose_rows(r + AHEAD_ROWS, 1)

@@ -60,14 +60,9 @@ def tile_synapsemodel_pa_kernel(tc, z, attention_out, Wz, bz, gz, bz_ln, w1_deq,
         nc.vector.memset(vrows1[:].bitcast(I32), 0)
         grows = const.tile([P, BANK], BF16, name="grows")
         nc.vector.memset(grows[:].bitcast(I32), 0)
-        vrows2 = const.tile([P, BANK], BF16, name="vrows2")
-        nc.vector.memset(vrows2[:].bitcast(I32), 0)
         nc.sync.dma_start(out=vrows1[0:2, :], in_=bz.rearrange("(a c) -> a c", a=2))
         nc.sync.dma_start(out=grows[0:2, :], in_=gz.rearrange("(a c) -> a c", a=2))
         nc.sync.dma_start(out=grows[2:4, :], in_=bz_ln.rearrange("(a c) -> a c", a=2))
-        nc.scalar.dma_start(out=vrows2[2:4, :], in_=b1.rearrange("(a c) -> a c", a=2))
-        nc.scalar.dma_start(out=vrows2[4:6, :], in_=g1.rearrange("(a c) -> a c", a=2))
-        nc.scalar.dma_start(out=vrows2[6:8, :], in_=b1_ln.rearrange("(a c) -> a c", a=2))
 
         zq = keep.tile([P, TILES * 512], U32, name="zq", align_bytes=64)
         zs = keep.tile([P, TILES * 512], U8, name="zs", align_bytes=64)
@@ -85,6 +80,9 @@ def tile_synapsemodel_pa_kernel(tc, z, attention_out, Wz, bz, gz, bz_ln, w1_deq,
 
         live = {}
 
+        def spread(i):
+            nc.sync.dma_start(out=bc[:, i * H:(i + 1) * H], in_=(bz, b1, g1, b1_ln)[i].partition_broadcast(P))
+
         def load(kind, idx):
             if kind == "a":
                 t = rawa.tile([P, H], BF16, tag="rawa")
@@ -100,29 +98,27 @@ def tile_synapsemodel_pa_kernel(tc, z, attention_out, Wz, bz, gz, bz_ln, w1_deq,
             nc.sync.dma_start(out=t[:], in_=src)
             live[("raw", kind, idx)] = t
 
-        def spread_row(r):
+        def spread_bias(half):
             pb = ps_t.tile([P, BANK], F32, tag="tp")
             nc.tensor.matmul(
-                pb[:], lhsT=identb[:, r:r + 1].to_broadcast([P, P]), rhs=(vrows1 if r < 2 else vrows2)[:],
-                start=True, stop=True,
+                pb[:], lhsT=identb[:, half:half + 1].to_broadcast([P, P]), rhs=vrows1[:], start=True, stop=True
             )
-            dst = bc[:, r * BANK:(r + 1) * BANK]
-            if r < 2:
-                nc.vector.tensor_copy(
-                    out=dst.rearrange("p (t q) -> p t q", t=4),
-                    in_=pb[:].rearrange("p (q t) -> p t q", t=4),
-                )
-            else:
-                nc.vector.tensor_copy(out=dst, in_=pb[:])
+            nc.vector.tensor_copy(
+                out=bc[:, half * BANK:(half + 1) * BANK].rearrange("p (t q) -> p t q", t=4),
+                in_=pb[:].rearrange("p (q t) -> p t q", t=4),
+            )
 
-        def gain_columns():
+        def sort_gains():
             g32 = const.tile([P, BANK], F32, name="g32")
             nc.vector.tensor_copy(
                 out=g32[:].rearrange("p (t q) -> p t q", t=4), in_=grows[:].rearrange("p (q t) -> p t q", t=4)
             )
+            live["g32"] = g32
+
+        def gain_columns():
             pg = ps_t.tile([P, BANK], F32, tag="tp")
             for t in range(4):
-                nc.tensor.transpose(pg[:, t * P:(t + 1) * P], g32[:, t * P:(t + 1) * P], ident[:])
+                nc.tensor.transpose(pg[:, t * P:(t + 1) * P], live["g32"][:, t * P:(t + 1) * P], ident[:])
             nc.vector.tensor_copy(
                 out=gb[:].rearrange("p (w a t) -> p w a t", w=2, t=4),
                 in_=pg[:].rearrange("p (t r) -> p t r", t=4)[:, :, 0:4].rearrange("p t (w a) -> p w a t", w=2),
@@ -304,16 +300,18 @@ def tile_synapsemodel_pa_kernel(tc, z, attention_out, Wz, bz, gz, bz_ln, w1_deq,
                     load("w", j)
                 if j % 2 == 0 and r + AHEAD_A >= 0:
                     load("a", r + AHEAD_A)
+            if -4 <= r <= -2:
+                spread(r + 5)
+
+        spread_bias(0)
+        spread_bias(1)
+        sort_gains()
 
         for j in range(TILES):
             transpose_words("W", j, 0)
             transpose_words("W", j, 1)
             if j == 1:
-                spread_row(0)
-                spread_row(1)
                 gain_columns()
-            if j >= 2:
-                spread_row(j)
             if j == 4:
                 quantise_weights("W", 0)
 

@@ -20,13 +20,12 @@ BANK = 512
 PASSES = D_IN // 512
 TILES = N_TOK // P
 LN_EPS = 1e-5
-FLOPS = 2 * N_TOK * D_IN * H + 2 * N_TOK * D_IN * H
-
 AHEAD_Z = 5
 AHEAD_M1 = 4
 AHEAD_A = 3
 AHEAD_ROWS = 2
-DRAIN_ROUNDS = 2
+DRAIN_ROUNDS = 4
+FLOPS = 2 * N_TOK * D_IN * H + 2 * N_TOK * D_IN * H
 
 
 def tile_synapsemodel_pa_kernel(tc, z, attention_out, Wz, bz, gz, bz_ln, w1_deq, b1, g1, b1_ln, out):
@@ -80,9 +79,6 @@ def tile_synapsemodel_pa_kernel(tc, z, attention_out, Wz, bz, gz, bz_ln, w1_deq,
 
         live = {}
 
-        def spread(i):
-            nc.sync.dma_start(out=bc[:, i * H:(i + 1) * H], in_=(bz, b1, g1, b1_ln)[i].partition_broadcast(P))
-
         def load(kind, idx):
             if kind == "a":
                 t = rawa.tile([P, H], BF16, tag="rawa")
@@ -98,88 +94,52 @@ def tile_synapsemodel_pa_kernel(tc, z, attention_out, Wz, bz, gz, bz_ln, w1_deq,
             nc.sync.dma_start(out=t[:], in_=src)
             live[("raw", kind, idx)] = t
 
-        def spread_bias(half):
-            pb = ps_t.tile([P, BANK], F32, tag="tp")
-            nc.tensor.matmul(
-                pb[:], lhsT=identb[:, half:half + 1].to_broadcast([P, P]), rhs=vrows1[:], start=True, stop=True
-            )
-            nc.vector.tensor_copy(
-                out=bc[:, half * BANK:(half + 1) * BANK].rearrange("p (t q) -> p t q", t=4),
-                in_=pb[:].rearrange("p (q t) -> p t q", t=4),
-            )
+        def spread(i):
+            nc.sync.dma_start(out=bc[:, i * H:(i + 1) * H], in_=(bz, b1, g1, b1_ln)[i].partition_broadcast(P))
 
-        def sort_gains():
-            g32 = const.tile([P, BANK], F32, name="g32")
-            nc.vector.tensor_copy(
-                out=g32[:].rearrange("p (t q) -> p t q", t=4), in_=grows[:].rearrange("p (q t) -> p t q", t=4)
-            )
-            live["g32"] = g32
-
-        def gain_columns():
-            pg = ps_t.tile([P, BANK], F32, tag="tp")
-            for t in range(4):
-                nc.tensor.transpose(pg[:, t * P:(t + 1) * P], live["g32"][:, t * P:(t + 1) * P], ident[:])
-            nc.vector.tensor_copy(
-                out=gb[:].rearrange("p (w a t) -> p w a t", w=2, t=4),
-                in_=pg[:].rearrange("p (t r) -> p t r", t=4)[:, :, 0:4].rearrange("p t (w a) -> p w a t", w=2),
-            )
-
-        def transpose_words(kind, idx, b):
-            if not 0 <= idx < TILES:
-                return
+        def tr(kind, idx, b):
             words = live[("raw", kind, idx)][:].bitcast(F32)
-            xt = ps_t.tile([P, BANK], F32, tag="tp")
+            xt = ps_t.tile([P, BANK], F32, tag="tp", name="xt")
             for s in range(4):
                 c0 = (2 * b + s // 2) * 256
                 nc.tensor.transpose(xt[:, s * P:(s + 1) * P], words[:, c0 + s % 2:c0 + 256:2], ident[:])
-            src = xt[:].rearrange("p (g u r) -> p g r u", g=2, u=2)
+            live[("xt", kind, idx, b)] = xt
+
+        def cp(kind, idx, b, eng):
+            src = live[("xt", kind, idx, b)][:].rearrange("p (g u r) -> p g r u", g=2, u=2)
             if kind in ("W", "w"):
                 key = ("grp", kind, idx // 4)
                 if key not in live:
-                    grouped_w = stagew.tile([P, 4 * D_IN], BF16, tag="grpw", align_bytes=64)
-                    live[key] = grouped_w
+                    live[key] = stagew.tile([P, 4 * D_IN], BF16, tag="grpw", align_bytes=64, name="grpw")
                 dst = live[key][:].bitcast(F32).rearrange("p (g j r u) -> p g j r u", g=4, j=4, u=2)[
                     :, 2 * b:2 * b + 2, idx % 4
                 ]
-                if b == 1:
-                    nc.vector.tensor_copy(out=dst, in_=src)
-                else:
-                    nc.scalar.copy(out=dst, in_=src)
             else:
                 key = ("grp", kind, idx)
                 if key not in live:
                     if kind == "a":
-                        grouped = stage.tile([P, H], BF16, tag="grpa", align_bytes=64)
+                        live[key] = stage.tile([P, H], BF16, tag="grpa", align_bytes=64, name="grpa")
                     else:
-                        grouped = stage.tile([P, D_IN], BF16, tag="grp", align_bytes=64)
-                    live[key] = grouped
-                dst = live[key][:].bitcast(F32)[:, b * BANK:(b + 1) * BANK].rearrange(
-                    "p (g r u) -> p g r u", g=2, u=2
-                )
-                nc.scalar.copy(out=dst, in_=src)
+                        live[key] = stage.tile([P, D_IN], BF16, tag="grp", align_bytes=64, name="grp")
+                dst = live[key][:].bitcast(F32)[:, b * BANK:(b + 1) * BANK].rearrange("p (g r u) -> p g r u", g=2, u=2)
+            eng(out=dst, in_=src)
 
-        def quantise_weights(kind, half):
+        def qw(kind, half, g):
             cq, cs = (wq, ws) if kind == "W" else (vq, vs)
-            for g in range(PASSES):
-                sl = slice(g * H + half * BANK, g * H + (half + 1) * BANK)
-                nc.vector.quantize_mx(
-                    out=cq[:, sl].bitcast(FP8X4), scales=cs[:, sl],
-                    in_=live[("grp", kind, half)][:, g * D_IN:(g + 1) * D_IN],
-                )
+            sl = slice(g * H + half * BANK, g * H + (half + 1) * BANK)
+            nc.vector.quantize_mx(out=cq[:, sl].bitcast(FP8X4), scales=cs[:, sl], in_=live[("grp", kind, half)][:, g * D_IN:(g + 1) * D_IN])
 
-        def quantise_rows(kind, idx):
-            if not 0 <= idx < TILES:
-                return
+        def qr(kind, idx):
             words = 512 if kind == "z" else 256
             cq, cs = (zq, zs) if kind == "z" else (aq, ascl)
             sl = slice(idx * words, (idx + 1) * words)
             nc.vector.quantize_mx(out=cq[:, sl].bitcast(FP8X4), scales=cs[:, sl], in_=live[("grp", kind, idx)][:])
 
-        def mx_group(stg, i, n):
-            if not 0 <= i < TILES:
-                return
-            acc = ps_a.tile([P, BANK], F32, tag="acc")
-            for g in range(PASSES):
+        def mx(stg, i, n, first=0, last=4):
+            if first == 0:
+                live[("acc", stg, i, n)] = ps_a.tile([P, BANK], F32, tag="acc", name="acc")
+            acc = live[("acc", stg, i, n)]
+            for g in range(first, last):
                 if stg == 1:
                     c0 = i * 512 + g * P
                     lq, ls, rq, rs = zq, zs, wq, ws
@@ -189,106 +149,125 @@ def tile_synapsemodel_pa_kernel(tc, z, attention_out, Wz, bz, gz, bz_ln, w1_deq,
                     rq, rs = vq, vs
                 sl = slice(c0, c0 + P)
                 sr = slice(g * H + n * BANK, g * H + (n + 1) * BANK)
-                nc.tensor.matmul_mx(
-                    out=acc[:], lhsT=lq[:, sl].bitcast(FP8X4), lhsT_scale=ls[:, sl],
-                    rhs=rq[:, sr].bitcast(FP8X4), rhs_scale=rs[:, sr], start=(g == 0), stop=(g == PASSES - 1),
-                )
+                nc.tensor.matmul_mx(out=acc[:], lhsT=lq[:, sl].bitcast(FP8X4), lhsT_scale=ls[:, sl], rhs=rq[:, sr].bitcast(FP8X4), rhs_scale=rs[:, sr], start=(g == 0), stop=(g == PASSES - 1))
+
+        def drain(stg, i, n):
             if n == 0:
-                if stg == 1:
-                    y = rows1.tile([P, H], F32, tag="y1")
-                else:
-                    y = rows2.tile([P, H], F32, tag="y2")
-                sums = small.tile([P, 2], F32, tag="sums")
-                live[("y", stg, i)] = y
-                live[("sums", stg, i)] = sums
+                live[("y", stg, i)] = (rows1 if stg == 1 else rows2).tile([P, H], F32, tag="y1" if stg == 1 else "y2", name="y")
+                live[("sums", stg, i)] = small.tile([P, 2], F32, tag="sums", name="sums")
             off = (stg - 1) * H + n * BANK
             nc.vector.scalar_tensor_tensor(
-                out=live[("y", stg, i)][:, n * BANK:(n + 1) * BANK], in0=acc[:], scalar=1.0,
-                in1=bc[:, off:off + BANK], op0=ALU.mult, op1=ALU.add, accum_out=live[("sums", stg, i)][:, n:n + 1],
-            )
+                out=live[("y", stg, i)][:, n * BANK:(n + 1) * BANK], in0=live[("acc", stg, i, n)][:], scalar=1.0,
+                in1=bc[:, off:off + BANK], op0=ALU.mult, op1=ALU.add, accum_out=live[("sums", stg, i)][:, n:n + 1])
 
-        def stats(stg, i):
-            if not 0 <= i < TILES:
-                return
+        def nmean_(stg, i):
             junk2 = small.tile([P, 2], F32, tag="junk2")
-            nmean = small.tile([P, 1], F32, tag="nmean")
-            nc.scalar.activation(
-                out=junk2[:], in_=live[("sums", stg, i)][:], func=ACT.Identity, scale=-1.0 / H, accum_out=nmean[:]
-            )
+            live[("nmean", stg, i)] = small.tile([P, 1], F32, tag="nmean", name="nmean")
+            nc.scalar.activation(out=junk2[:], in_=live[("sums", stg, i)][:], func=ACT.Identity, scale=-1.0 / H, accum_out=live[("nmean", stg, i)][:])
+
+        def square_(stg, i):
             junk = junkp.tile([P, H], BF16, tag="junk")
-            ssq = small.tile([P, 1], F32, tag="ssq")
-            nc.scalar.activation(
-                out=junk[:], in_=live[("y", stg, i)][:], func=ACT.Square, bias=nmean[:], scale=1.0, accum_out=ssq[:]
-            )
-            veps = small.tile([P, 1], F32, tag="veps")
-            nc.scalar.activation(out=veps[:], in_=ssq[:], func=ACT.Identity, scale=1.0 / H, bias=eps[:])
-            live[("nmean", stg, i)] = nmean
-            live[("veps", stg, i)] = veps
+            live[("ssq", stg, i)] = small.tile([P, 1], F32, tag="ssq", name="ssq")
+            nc.scalar.activation(out=junk[:], in_=live[("y", stg, i)][:], func=ACT.Square, bias=live[("nmean", stg, i)][:], scale=1.0, accum_out=live[("ssq", stg, i)][:])
 
-        def rstd_of(stg, i):
-            if not 0 <= i < TILES:
-                return
-            rstd = small.tile([P, 1], F32, tag="rstd")
-            nc.gpsimd.tensor_tensor(out=rstd[:], in0=live[("veps", stg, i)][:], in1=mhalf[:], op=ALU.pow)
-            live[("rstd", stg, i)] = rstd
-            if stg == 1:
-                y = live[("y", 1, i)]
-                nc.gpsimd.tensor_scalar(
-                    out=y[:], in0=y[:], scalar1=live[("nmean", 1, i)][:], scalar2=rstd[:], op0=ALU.add, op1=ALU.mult
-                )
+        def veps_(stg, i):
+            live[("veps", stg, i)] = small.tile([P, 1], F32, tag="veps", name="veps")
+            nc.scalar.activation(out=live[("veps", stg, i)][:], in_=live[("ssq", stg, i)][:], func=ACT.Identity, scale=1.0 / H, bias=eps[:])
 
-        def transpose_rows(i, g):
-            if not 0 <= i < TILES:
-                return
-            tp = ps_t.tile([P, BANK], F32, tag="tp")
+        def pow_(stg, i):
+            live[("rstd", stg, i)] = small.tile([P, 1], F32, tag="rstd", name="rstd")
+            nc.gpsimd.tensor_tensor(out=live[("rstd", stg, i)][:], in0=live[("veps", stg, i)][:], in1=mhalf[:], op=ALU.pow)
+
+        def norm(i, eng):
+            y = live[("y", 1, i)]
+            eng(out=y[:], in0=y[:], scalar1=live[("nmean", 1, i)][:], scalar2=live[("rstd", 1, i)][:], op0=ALU.add, op1=ALU.mult)
+
+        def rows_tr(i, g):
+            live[("tp", i, g)] = ps_t.tile([P, BANK], F32, tag="tp", name="tp")
             for t in range(4):
                 j = 4 * g + t
-                nc.tensor.transpose(tp[:, t * P:(t + 1) * P], live[("y", 1, i)][:, j * P:(j + 1) * P], ident[:])
+                nc.tensor.transpose(live[("tp", i, g)][:, t * P:(t + 1) * P], live[("y", 1, i)][:, j * P:(j + 1) * P], ident[:])
+
+        def rows_out(i, g):
             if g == 0:
-                planar = plan.tile([P, H], BF16, tag="planar")
-                live[("planar", i)] = planar
+                live[("planar", i)] = plan.tile([P, H], BF16, tag="planar", name="planar")
             for t in range(4):
                 j = 4 * g + t
-                nc.scalar.activation(
-                    out=live[("planar", i)][:, j * P:(j + 1) * P], in_=tp[:, t * P:(t + 1) * P], func=ACT.Identity,
-                    scale=gb[:, j:j + 1], bias=gb[:, 8 + j:9 + j],
-                )
+                nc.scalar.activation(out=live[("planar", i)][:, j * P:(j + 1) * P], in_=live[("tp", i, g)][:, t * P:(t + 1) * P], func=ACT.Identity, scale=gb[:, j:j + 1], bias=gb[:, 8 + j:9 + j])
 
         def regroup(i):
-            if not 0 <= i < TILES:
-                return
-            gp = plan.tile([P, H], BF16, tag="gp", align_bytes=64)
-            nc.vector.tensor_copy(
-                out=gp[:].rearrange("p (g c t) -> p g c t", g=2, t=4),
-                in_=live[("planar", i)][:].rearrange("p (g t c) -> p g c t", g=2, t=4),
-            )
+            live[("gp", i)] = plan.tile([P, H], BF16, tag="gp", align_bytes=64, name="gp")
+            nc.vector.tensor_copy(out=live[("gp", i)][:].rearrange("p (g c t) -> p g c t", g=2, t=4), in_=live[("planar", i)][:].rearrange("p (g t c) -> p g c t", g=2, t=4))
+
+        def quant_p(i):
             sl = slice(i * 256, (i + 1) * 256)
-            nc.vector.quantize_mx(out=pq[:, sl].bitcast(FP8X4), scales=pscl[:, sl], in_=gp[:])
+            nc.vector.quantize_mx(out=pq[:, sl].bitcast(FP8X4), scales=pscl[:, sl], in_=live[("gp", i)][:])
 
         def gain(i):
-            if not 0 <= i < TILES:
-                return
-            t2 = rows3.tile([P, H], F32, tag="t2")
-            nc.vector.scalar_tensor_tensor(
-                out=t2[:], in0=live[("y", 2, i)][:], scalar=live[("nmean", 2, i)][:], in1=bc[:, 2 * H:3 * H],
-                op0=ALU.add, op1=ALU.mult,
-            )
-            live[("t2", i)] = t2
+            live[("t2", i)] = rows3.tile([P, H], F32, tag="t2", name="t2")
+            nc.vector.scalar_tensor_tensor(out=live[("t2", i)][:], in0=live[("y", 2, i)][:], scalar=live[("nmean", 2, i)][:], in1=bc[:, 2 * H:3 * H], op0=ALU.add, op1=ALU.mult)
 
         def shift(i):
-            if not 0 <= i < TILES:
-                return
             t2 = live[("t2", i)]
-            nc.vector.scalar_tensor_tensor(
-                out=t2[:], in0=t2[:], scalar=live[("rstd", 2, i)][:], in1=bc[:, 3 * H:4 * H], op0=ALU.mult, op1=ALU.add
-            )
+            nc.vector.scalar_tensor_tensor(out=t2[:], in0=t2[:], scalar=live[("rstd", 2, i)][:], in1=bc[:, 3 * H:4 * H], op0=ALU.mult, op1=ALU.add)
 
-        def gelu_store(i):
-            if not 0 <= i < TILES:
-                return
-            t2 = live[("t2", i)]
-            nc.scalar.activation(out=t2[:], in_=t2[:], func=ACT.Gelu)
-            nc.sync.dma_start(out=out[i * P:(i + 1) * P, :], in_=t2[:])
+        def gelu(i):
+            nc.scalar.activation(out=live[("t2", i)][:], in_=live[("t2", i)][:], func=ACT.Gelu)
+
+        def store(i):
+            nc.sync.dma_start(out=out[i * P:(i + 1) * P, :], in_=live[("t2", i)][:])
+
+        def bias(half):
+            pb = ps_t.tile([P, BANK], F32, tag="tp")
+            nc.tensor.matmul(pb[:], lhsT=identb[:, half:half + 1].to_broadcast([P, P]), rhs=vrows1[:], start=True, stop=True)
+            nc.vector.tensor_copy(out=bc[:, half * BANK:(half + 1) * BANK].rearrange("p (t q) -> p t q", t=4), in_=pb[:].rearrange("p (q t) -> p t q", t=4))
+
+        def sort_gains():
+            live["g32"] = const.tile([P, BANK], F32, name="g32")
+            nc.vector.tensor_copy(out=live["g32"][:].rearrange("p (t q) -> p t q", t=4), in_=grows[:].rearrange("p (q t) -> p t q", t=4))
+
+        def gain_columns():
+            pg = ps_t.tile([P, BANK], F32, tag="tp")
+            for t in range(4):
+                nc.tensor.transpose(pg[:, t * P:(t + 1) * P], live["g32"][:, t * P:(t + 1) * P], ident[:])
+            nc.vector.tensor_copy(out=gb[:].rearrange("p (w a t) -> p w a t", w=2, t=4), in_=pg[:].rearrange("p (t r) -> p t r", t=4)[:, :, 0:4].rearrange("p t (w a) -> p w a t", w=2))
+
+        S, V = nc.scalar.copy, nc.vector.tensor_copy
+
+        def on(fn, *args):
+            if 0 <= args[-1] < TILES:
+                fn(*args)
+
+        def words_in(kind, b, i):
+            tr(kind, i, b)
+
+        def words_out(kind, b, i):
+            cp(kind, i, b, V if kind in ("W", "w") and b else S)
+
+        def words(kind, b, i):
+            words_in(kind, b, i)
+            words_out(kind, b, i)
+
+        def m1(n, i):
+            mx(1, i, n)
+
+        def m2(n, i):
+            mx(2, i, n)
+
+        def d1(n, i):
+            drain(1, i, n)
+
+        def d2(n, i):
+            drain(2, i, n)
+
+        def r_in(g, i):
+            rows_tr(i, g)
+
+        def r_out(g, i):
+            rows_out(i, g)
+
+        def norm_rows(i):
+            norm(i, nc.gpsimd.tensor_scalar)
 
         for j in range(TILES):
             load("W", j)
@@ -302,45 +281,59 @@ def tile_synapsemodel_pa_kernel(tc, z, attention_out, Wz, bz, gz, bz_ln, w1_deq,
                     load("a", r + AHEAD_A)
             if -4 <= r <= -2:
                 spread(r + 5)
-
-        spread_bias(0)
-        spread_bias(1)
+        bias(0)
+        bias(1)
         sort_gains()
-
         for j in range(TILES):
-            transpose_words("W", j, 0)
-            transpose_words("W", j, 1)
+            words("W", 0, j)
+            words("W", 1, j)
             if j == 1:
                 gain_columns()
             if j == 4:
-                quantise_weights("W", 0)
+                for g in range(PASSES):
+                    qw("W", 0, g)
 
         for r in range(-AHEAD_Z, TILES + DRAIN_ROUNDS):
-            w_first = 2 * (r + AHEAD_Z)
-            mx_group(2, r, 0)
-            regroup(r + 1)
-            transpose_words("z", r + AHEAD_Z, 0)
-            rstd_of(2, r - 1)
-            transpose_words("z", r + AHEAD_Z, 1)
-            if w_first == 0:
-                quantise_weights("W", 1)
-            elif w_first in (4, 8):
-                quantise_weights("w", w_first // 4 - 1)
-            transpose_words("w", w_first, 0)
-            transpose_words("w", w_first, 1)
-            mx_group(2, r, 1)
-            stats(1, r + AHEAD_M1 - 1)
-            rstd_of(1, r + AHEAD_M1 - 1)
-            gelu_store(r - 2)
-            transpose_words("a", r + AHEAD_A, 0)
-            mx_group(1, r + AHEAD_M1, 0)
-            transpose_rows(r + AHEAD_ROWS, 0)
-            transpose_words("w", w_first + 1, 0)
-            transpose_words("w", w_first + 1, 1)
-            quantise_rows("z", r + AHEAD_Z)
-            stats(2, r)
-            mx_group(1, r + AHEAD_M1, 1)
-            quantise_rows("a", r + AHEAD_A)
-            shift(r - 1)
-            gain(r)
-            transpose_rows(r + AHEAD_ROWS, 1)
+            u = 2 * (r + AHEAD_Z)
+            on(words, "z", 1, r + 5)
+            on(words, "z", 0, r + 5)
+            on(veps_, 2, r - 1)
+            on(pow_, 2, r - 1)
+            on(d2, 0, r)
+            if u == 0:
+                for g in range(PASSES):
+                    qw("W", 1, g)
+            elif u in (4, 8):
+                for g in range(PASSES):
+                    qw("w", u // 4 - 1, g)
+            on(words, "w", 1, u)
+            on(regroup, r + 1)
+            on(m2, 1, r)
+            on(square_, 1, r + 3)
+            on(words, "w", 0, u)
+            on(veps_, 1, r + 3)
+            on(gelu, r - 2)
+            on(pow_, 1, r + 3)
+            on(d2, 1, r)
+            on(quant_p, r + 1)
+            on(words, "a", 0, r + 3)
+            on(qr, "z", r + 5)
+            on(norm_rows, r + 3)
+            on(m1, 0, r + 4)
+            on(r_in, 0, r + 2)
+            on(d1, 0, r + 4)
+            on(store, r - 3)
+            on(words, "w", 1, u + 1)
+            on(nmean_, 2, r)
+            on(words, "w", 0, u + 1)
+            on(m1, 1, r + 4)
+            on(r_out, 0, r + 2)
+            on(shift, r - 1)
+            on(r_in, 1, r + 2)
+            on(square_, 2, r)
+            on(d1, 1, r + 4)
+            on(nmean_, 1, r + 4)
+            on(gain, r)
+            on(m2, 0, r + 1)
+            on(qr, "a", r + 3)
+            on(r_out, 1, r + 2)

@@ -78,6 +78,7 @@ def tile_synapsemodel_pa_kernel(tc, z, attention_out, Wz, bz, gz, bz_ln, w1_deq,
         wz_rows = Wz.rearrange("(a q t) k -> a t q k", q=P, t=4)
 
         live = {}
+        S, V = nc.scalar.copy, nc.vector.tensor_copy
 
         def load(kind, idx):
             if kind == "a":
@@ -197,7 +198,7 @@ def tile_synapsemodel_pa_kernel(tc, z, attention_out, Wz, bz, gz, bz_ln, w1_deq,
 
         def regroup(i):
             live[("gp", i)] = plan.tile([P, H], BF16, tag="gp", align_bytes=64, name="gp")
-            nc.vector.tensor_copy(out=live[("gp", i)][:].rearrange("p (g c t) -> p g c t", g=2, t=4), in_=live[("planar", i)][:].rearrange("p (g t c) -> p g c t", g=2, t=4))
+            (S if i >= TILES - 2 else V)(out=live[("gp", i)][:].rearrange("p (g c t) -> p g c t", g=2, t=4), in_=live[("planar", i)][:].rearrange("p (g t c) -> p g c t", g=2, t=4))
 
         def quant_p(i):
             sl = slice(i * 256, (i + 1) * 256)
@@ -207,15 +208,22 @@ def tile_synapsemodel_pa_kernel(tc, z, attention_out, Wz, bz, gz, bz_ln, w1_deq,
             live[("t2", i)] = rows3.tile([P, H], F32, tag="t2", name="t2")
             nc.vector.scalar_tensor_tensor(out=live[("t2", i)][:], in0=live[("y", 2, i)][:], scalar=live[("nmean", 2, i)][:], in1=bc[:, 2 * H:3 * H], op0=ALU.add, op1=ALU.mult)
 
+        def parts(i):
+            n = 2 if i == TILES - 1 else 1
+            return [slice(k * H // n, (k + 1) * H // n) for k in range(n)]
+
         def shift(i):
             t2 = live[("t2", i)]
-            nc.vector.scalar_tensor_tensor(out=t2[:], in0=t2[:], scalar=live[("rstd", 2, i)][:], in1=bc[:, 3 * H:4 * H], op0=ALU.mult, op1=ALU.add)
+            for c in parts(i):
+                nc.vector.scalar_tensor_tensor(out=t2[:, c], in0=t2[:, c], scalar=live[("rstd", 2, i)][:], in1=bc[:, 3 * H + c.start:3 * H + c.stop], op0=ALU.mult, op1=ALU.add)
 
         def gelu(i):
-            nc.scalar.activation(out=live[("t2", i)][:], in_=live[("t2", i)][:], func=ACT.Gelu)
+            for c in parts(i):
+                nc.scalar.activation(out=live[("t2", i)][:, c], in_=live[("t2", i)][:, c], func=ACT.Gelu)
 
         def store(i):
-            nc.sync.dma_start(out=out[i * P:(i + 1) * P, :], in_=live[("t2", i)][:])
+            for c in parts(i):
+                nc.sync.dma_start(out=out[i * P:(i + 1) * P, c], in_=live[("t2", i)][:, c])
 
         def bias(half):
             pb = ps_t.tile([P, BANK], F32, tag="tp")
@@ -232,8 +240,6 @@ def tile_synapsemodel_pa_kernel(tc, z, attention_out, Wz, bz, gz, bz_ln, w1_deq,
                 nc.tensor.transpose(pg[:, t * P:(t + 1) * P], live["g32"][:, t * P:(t + 1) * P], ident[:])
             nc.vector.tensor_copy(out=gb[:].rearrange("p (w a t) -> p w a t", w=2, t=4), in_=pg[:].rearrange("p (t r) -> p t r", t=4)[:, :, 0:4].rearrange("p t (w a) -> p w a t", w=2))
 
-        S, V = nc.scalar.copy, nc.vector.tensor_copy
-
         def on(fn, *args):
             if 0 <= args[-1] < TILES:
                 fn(*args)
@@ -242,7 +248,7 @@ def tile_synapsemodel_pa_kernel(tc, z, attention_out, Wz, bz, gz, bz_ln, w1_deq,
             tr(kind, i, b)
 
         def words_out(kind, b, i):
-            cp(kind, i, b, V if kind in ("W", "w") and b else S)
+            cp(kind, i, b, V if kind in ("W", "w") and b and i % 2 else S)
 
         def words(kind, b, i):
             words_in(kind, b, i)
@@ -295,45 +301,45 @@ def tile_synapsemodel_pa_kernel(tc, z, attention_out, Wz, bz, gz, bz_ln, w1_deq,
 
         for r in range(-AHEAD_Z, TILES + DRAIN_ROUNDS):
             u = 2 * (r + AHEAD_Z)
-            on(words, "z", 1, r + 5)
             on(words, "z", 0, r + 5)
-            on(veps_, 2, r - 1)
-            on(pow_, 2, r - 1)
-            on(d2, 0, r)
+            on(square_, 2, r - 1)
+            on(shift, r - 2)
+            on(m2, 0, r)
+            on(words, "a", 0, r + 3)
+            on(qr, "a", r + 1)
             if u == 0:
                 for g in range(PASSES):
                     qw("W", 1, g)
             elif u in (4, 8):
                 for g in range(PASSES):
                     qw("w", u // 4 - 1, g)
-            on(words, "w", 1, u)
-            on(regroup, r + 1)
-            on(m2, 1, r)
-            on(square_, 1, r + 3)
+            on(words, "z", 1, r + 5)
+            on(veps_, 2, r - 1)
             on(words, "w", 0, u)
+            on(square_, 1, r + 3)
             on(veps_, 1, r + 3)
-            on(gelu, r - 2)
+            on(gain, r - 1)
+            on(d2, 0, r)
+            on(pow_, 2, r - 1)
+            on(regroup, r + 1)
             on(pow_, 1, r + 3)
+            on(m2, 1, r)
             on(d2, 1, r)
             on(quant_p, r + 1)
-            on(words, "a", 0, r + 3)
-            on(qr, "z", r + 5)
-            on(norm_rows, r + 3)
+            on(words, "w", 1, u)
             on(m1, 0, r + 4)
+            on(qr, "z", r + 5)
+            on(words, "w", 1, u + 1)
+            on(words, "w", 0, u + 1)
             on(r_in, 0, r + 2)
             on(d1, 0, r + 4)
-            on(store, r - 3)
-            on(words, "w", 1, u + 1)
-            on(nmean_, 2, r)
-            on(words, "w", 0, u + 1)
+            on(gelu, r - 2)
             on(m1, 1, r + 4)
+            on(nmean_, 2, r)
+            on(norm_rows, r + 3)
             on(r_out, 0, r + 2)
-            on(shift, r - 1)
-            on(r_in, 1, r + 2)
-            on(square_, 2, r)
             on(d1, 1, r + 4)
-            on(nmean_, 1, r + 4)
-            on(gain, r)
-            on(m2, 0, r + 1)
-            on(qr, "a", r + 3)
+            on(r_in, 1, r + 2)
+            on(store, r - 2)
             on(r_out, 1, r + 2)
+            on(nmean_, 1, r + 4)

@@ -47,6 +47,10 @@ def tile_synapsemodel_pa_kernel(tc, z, attention_out, Wz, bz, gz, bz_ln, w1_deq,
         ps_a = ctx.enter_context(tc.psum_pool(name="ps_a", bufs=3))
         ctx.enter_context(tc.manual_schedule())
 
+        vrows1 = const.tile([P, BANK], BF16, name="vrows1")
+        nc.vector.memset(vrows1[:].bitcast(I32), 0)
+        grows = const.tile([P, BANK], BF16, name="grows")
+        nc.vector.memset(grows[:].bitcast(I32), 0)
         ident = const.tile([P, P], F32, name="ident")
         make_identity(nc, ident[:])
         identb = const.tile([P, P], BF16, name="identb")
@@ -55,13 +59,6 @@ def tile_synapsemodel_pa_kernel(tc, z, attention_out, Wz, bz, gz, bz_ln, w1_deq,
         nc.vector.memset(mhalf[:], -0.5)
         eps = const.tile([P, 1], F32, name="eps")
         nc.vector.memset(eps[:], LN_EPS)
-        vrows1 = const.tile([P, BANK], BF16, name="vrows1")
-        nc.vector.memset(vrows1[:].bitcast(I32), 0)
-        grows = const.tile([P, BANK], BF16, name="grows")
-        nc.vector.memset(grows[:].bitcast(I32), 0)
-        nc.sync.dma_start(out=vrows1[0:2, :], in_=bz.rearrange("(a c) -> a c", a=2))
-        nc.sync.dma_start(out=grows[0:2, :], in_=gz.rearrange("(a c) -> a c", a=2))
-        nc.sync.dma_start(out=grows[2:4, :], in_=bz_ln.rearrange("(a c) -> a c", a=2))
 
         zq = keep.tile([P, TILES * 512], U32, name="zq", align_bytes=64)
         zs = keep.tile([P, TILES * 512], U8, name="zs", align_bytes=64)
@@ -277,6 +274,10 @@ def tile_synapsemodel_pa_kernel(tc, z, attention_out, Wz, bz, gz, bz_ln, w1_deq,
 
         for j in range(TILES):
             load("W", j)
+            if j == 0:
+                nc.sync.dma_start(out=vrows1[0:2, :], in_=bz.rearrange("(a c) -> a c", a=2))
+                nc.sync.dma_start(out=grows[0:2, :], in_=gz.rearrange("(a c) -> a c", a=2))
+                nc.sync.dma_start(out=grows[2:4, :], in_=bz_ln.rearrange("(a c) -> a c", a=2))
         for r in range(-AHEAD_Z, TILES - AHEAD_A):
             if r + AHEAD_Z < TILES:
                 load("z", r + AHEAD_Z)
@@ -285,14 +286,15 @@ def tile_synapsemodel_pa_kernel(tc, z, attention_out, Wz, bz, gz, bz_ln, w1_deq,
                     load("w", j)
                 if j % 2 == 0 and r + AHEAD_A >= 0:
                     load("a", r + AHEAD_A)
-            if -4 <= r <= -2:
-                spread(r + 5)
-        bias(0)
-        bias(1)
-        sort_gains()
+            if -2 <= r <= 0:
+                spread(r + 3)
         for j in range(TILES):
             words("W", 0, j)
             words("W", 1, j)
+            if j == 0:
+                bias(0)
+                bias(1)
+                sort_gains()
             if j == 1:
                 gain_columns()
             if j == 4:

@@ -49,8 +49,6 @@ def tile_synapsemodel_pa_kernel(tc, z, attention_out, Wz, bz, gz, bz_ln, w1_deq,
 
         vrows1 = const.tile([P, BANK], BF16, name="vrows1")
         nc.vector.memset(vrows1[:].bitcast(I32), 0)
-        grows = const.tile([P, BANK], BF16, name="grows")
-        nc.vector.memset(grows[:].bitcast(I32), 0)
         ident = const.tile([P, P], F32, name="ident")
         make_identity(nc, ident[:])
         identb = const.tile([P, P], BF16, name="identb")
@@ -89,7 +87,11 @@ def tile_synapsemodel_pa_kernel(tc, z, attention_out, Wz, bz, gz, bz_ln, w1_deq,
                     src = z[idx * P:(idx + 1) * P, :]
                 else:
                     src = w1_deq[idx * P:(idx + 1) * P, :]
-            nc.sync.dma_start(out=t[:], in_=src)
+            if kind == "W" and idx == 0:
+                for c in (slice(0, D_IN // 2), slice(D_IN // 2, D_IN)):
+                    nc.sync.dma_start(out=t[:, c], in_=src[:, c])
+            else:
+                nc.sync.dma_start(out=t[:], in_=src)
             live[("raw", kind, idx)] = t
 
         def spread(i):
@@ -227,15 +229,15 @@ def tile_synapsemodel_pa_kernel(tc, z, attention_out, Wz, bz, gz, bz_ln, w1_deq,
             nc.tensor.matmul(pb[:], lhsT=identb[:, half:half + 1].to_broadcast([P, P]), rhs=vrows1[:], start=True, stop=True)
             nc.vector.tensor_copy(out=bc[:, half * BANK:(half + 1) * BANK].rearrange("p (t q) -> p t q", t=4), in_=pb[:].rearrange("p (q t) -> p t q", t=4))
 
-        def sort_gains():
-            live["g32"] = const.tile([P, BANK], F32, name="g32")
-            nc.vector.tensor_copy(out=live["g32"][:].rearrange("p (t q) -> p t q", t=4), in_=grows[:].rearrange("p (q t) -> p t q", t=4))
+        def load_gains():
+            for w, vec in enumerate((gz, bz_ln)):
+                g16 = const.tile([P, 8], BF16, name="g16_%d" % w)
+                nc.sync.dma_start(out=g16[:].rearrange("p (a t) -> p a t", a=2), in_=vec.rearrange("(a q t) -> q a t", q=P, t=4))
+                live[("g16", w)] = g16
 
         def gain_columns():
-            pg = ps_t.tile([P, BANK], F32, tag="tp")
-            for t in range(4):
-                nc.tensor.transpose(pg[:, t * P:(t + 1) * P], live["g32"][:, t * P:(t + 1) * P], ident[:])
-            nc.vector.tensor_copy(out=gb[:].rearrange("p (w a t) -> p w a t", w=2, t=4), in_=pg[:].rearrange("p (t r) -> p t r", t=4)[:, :, 0:4].rearrange("p t (w a) -> p w a t", w=2))
+            for w in range(2):
+                nc.vector.tensor_copy(out=gb[:, 8 * w:8 * w + 8], in_=live[("g16", w)][:])
 
         def on(fn, *args):
             if 0 <= args[-1] < TILES:
@@ -276,8 +278,6 @@ def tile_synapsemodel_pa_kernel(tc, z, attention_out, Wz, bz, gz, bz_ln, w1_deq,
             load("W", j)
             if j == 0:
                 nc.sync.dma_start(out=vrows1[0:2, :], in_=bz.rearrange("(a c) -> a c", a=2))
-                nc.sync.dma_start(out=grows[0:2, :], in_=gz.rearrange("(a c) -> a c", a=2))
-                nc.sync.dma_start(out=grows[2:4, :], in_=bz_ln.rearrange("(a c) -> a c", a=2))
         for r in range(-AHEAD_Z, TILES - AHEAD_A):
             if r + AHEAD_Z < TILES:
                 load("z", r + AHEAD_Z)
@@ -286,6 +286,8 @@ def tile_synapsemodel_pa_kernel(tc, z, attention_out, Wz, bz, gz, bz_ln, w1_deq,
                     load("w", j)
                 if j % 2 == 0 and r + AHEAD_A >= 0:
                     load("a", r + AHEAD_A)
+            if r == -4:
+                load_gains()
             if -2 <= r <= 0:
                 spread(r + 3)
         for j in range(TILES):
@@ -294,54 +296,53 @@ def tile_synapsemodel_pa_kernel(tc, z, attention_out, Wz, bz, gz, bz_ln, w1_deq,
             if j == 0:
                 bias(0)
                 bias(1)
-                sort_gains()
-            if j == 1:
-                gain_columns()
             if j == 4:
                 for g in range(PASSES):
                     qw("W", 0, g)
 
         for r in range(-AHEAD_Z, TILES + DRAIN_ROUNDS):
             u = 2 * (r + AHEAD_Z)
+            if r == -AHEAD_ROWS:
+                gain_columns()
             on(words, "z", 0, r + 5)
-            on(square_, 2, r - 1)
-            on(shift, r - 2)
             on(m2, 0, r)
-            on(words, "a", 0, r + 3)
-            on(qr, "a", r + 1)
+            on(veps_, 2, r - 1)
+            on(gain, r - 1)
+            on(words, "z", 1, r + 5)
+            on(pow_, 2, r - 1)
+            on(d2, 0, r)
             if u == 0:
                 for g in range(PASSES):
                     qw("W", 1, g)
             elif u in (4, 8):
                 for g in range(PASSES):
                     qw("w", u // 4 - 1, g)
-            on(words, "z", 1, r + 5)
-            on(veps_, 2, r - 1)
-            on(words, "w", 0, u)
+            on(qr, "a", r + 2)
+            on(words, "w", 1, u)
             on(square_, 1, r + 3)
+            on(words, "a", 0, r + 3)
+            on(words, "w", 0, u)
             on(veps_, 1, r + 3)
-            on(gain, r - 1)
-            on(d2, 0, r)
-            on(pow_, 2, r - 1)
             on(regroup, r + 1)
-            on(pow_, 1, r + 3)
+            on(gelu, r - 2)
             on(m2, 1, r)
+            on(pow_, 1, r + 3)
+            on(store, r - 3)
             on(d2, 1, r)
             on(quant_p, r + 1)
-            on(words, "w", 1, u)
             on(m1, 0, r + 4)
             on(qr, "z", r + 5)
-            on(words, "w", 1, u + 1)
-            on(words, "w", 0, u + 1)
-            on(r_in, 0, r + 2)
-            on(d1, 0, r + 4)
-            on(gelu, r - 2)
-            on(m1, 1, r + 4)
             on(nmean_, 2, r)
-            on(norm_rows, r + 3)
+            on(r_in, 0, r + 2)
+            on(words, "w", 0, u + 1)
             on(r_out, 0, r + 2)
-            on(d1, 1, r + 4)
+            on(words, "w", 1, u + 1)
+            on(m1, 1, r + 4)
+            on(norm_rows, r + 3)
             on(r_in, 1, r + 2)
-            on(store, r - 2)
-            on(r_out, 1, r + 2)
+            on(square_, 2, r)
+            on(d1, 0, r + 4)
+            on(d1, 1, r + 4)
             on(nmean_, 1, r + 4)
+            on(r_out, 1, r + 2)
+            on(shift, r - 1)

@@ -47,14 +47,16 @@ def tile_synapsemodel_pa_kernel(tc, z, attention_out, Wz, bz, gz, bz_ln, w1_deq,
         ps_a = ctx.enter_context(tc.psum_pool(name="ps_a", bufs=3))
         ctx.enter_context(tc.manual_schedule())
 
+        mhalf = const.tile([P, 1], F32, name="mhalf")
+        nc.vector.memset(mhalf[:], -0.5)
+        table = const.tile([P, 1], F32, name="table")
+        nc.scalar.activation(out=table[:], in_=mhalf[:], func=ACT.Gelu)
         vrows1 = const.tile([P, BANK], BF16, name="vrows1")
         nc.vector.memset(vrows1[:].bitcast(I32), 0)
         ident = const.tile([P, P], F32, name="ident")
         make_identity(nc, ident[:])
         identb = const.tile([P, P], BF16, name="identb")
         nc.vector.tensor_copy(out=identb[:], in_=ident[:])
-        mhalf = const.tile([P, 1], F32, name="mhalf")
-        nc.vector.memset(mhalf[:], -0.5)
         eps = const.tile([P, 1], F32, name="eps")
         nc.vector.memset(eps[:], LN_EPS)
 
@@ -286,7 +288,7 @@ def tile_synapsemodel_pa_kernel(tc, z, attention_out, Wz, bz, gz, bz_ln, w1_deq,
                     load("w", j)
                 if j % 2 == 0 and r + AHEAD_A >= 0:
                     load("a", r + AHEAD_A)
-            if r == -4:
+            if r == -2:
                 load_gains()
             if -2 <= r <= 0:
                 spread(r + 3)

from contextlib import ExitStack

import concourse.mybir as mybir
from concourse.masks import make_identity

F32 = mybir.dt.float32
BF16 = mybir.dt.bfloat16
U32 = mybir.dt.uint32
U8 = mybir.dt.uint8
I32 = mybir.dt.int32
FP8X4 = mybir.dt.float8_e4m3fn_x4
ALU = mybir.AluOpType
ACT = mybir.ActivationFunctionType

P = 128
N_TOK = 1024
D_IN = 2048
H = 1024
BANK = 512
PASSES = D_IN // 512
TILES = N_TOK // P
LN_EPS = 1e-5
AHEAD_Z = 5
AHEAD_M1 = 4
AHEAD_A = 3
AHEAD_ROWS = 2
DRAIN_ROUNDS = 4
FLOPS = 2 * N_TOK * D_IN * H + 2 * N_TOK * D_IN * H


def tile_synapsemodel_pa_kernel(tc, z, attention_out, Wz, bz, gz, bz_ln, w1_deq, b1, g1, b1_ln, out):
    nc = tc.nc
    with ExitStack() as ctx:
        const = ctx.enter_context(tc.tile_pool(name="const", bufs=1))
        keep = ctx.enter_context(tc.tile_pool(name="keep", bufs=1))
        raw = ctx.enter_context(tc.tile_pool(name="raw", bufs=6))
        rawa = ctx.enter_context(tc.tile_pool(name="rawa", bufs=4))
        stage = ctx.enter_context(tc.tile_pool(name="stage", bufs=3))
        stagew = ctx.enter_context(tc.tile_pool(name="stagew", bufs=2))
        rows1 = ctx.enter_context(tc.tile_pool(name="rows1", bufs=4))
        rows2 = ctx.enter_context(tc.tile_pool(name="rows2", bufs=2))
        rows3 = ctx.enter_context(tc.tile_pool(name="rows3", bufs=3))
        junkp = ctx.enter_context(tc.tile_pool(name="junkp", bufs=1))
        plan = ctx.enter_context(tc.tile_pool(name="plan", bufs=2))
        small = ctx.enter_context(tc.tile_pool(name="small", bufs=8))
        ps_t = ctx.enter_context(tc.psum_pool(name="ps_t", bufs=5))
        ps_a = ctx.enter_context(tc.psum_pool(name="ps_a", bufs=3))
        ctx.enter_context(tc.manual_schedule())

        mhalf = const.tile([P, 1], F32, name="mhalf")
        nc.vector.memset(mhalf[:], -0.5)
        table = const.tile([P, 1], F32, name="table")
        nc.scalar.activation(out=table[:], in_=mhalf[:], func=ACT.Gelu)
        vrows1 = const.tile([P, BANK], BF16, name="vrows1")
        nc.vector.memset(vrows1[:].bitcast(I32), 0)
        ident = const.tile([P, P], F32, name="ident")
        make_identity(nc, ident[:])
        identb = const.tile([P, P], BF16, name="identb")
        nc.vector.tensor_copy(out=identb[:], in_=ident[:])
        eps = const.tile([P, 1], F32, name="eps")
        nc.vector.memset(eps[:], LN_EPS)

        zq = keep.tile([P, TILES * 512], U32, name="zq", align_bytes=64)
        zs = keep.tile([P, TILES * 512], U8, name="zs", align_bytes=64)
        wq = keep.tile([P, PASSES * H], U32, name="wq", align_bytes=64)
        ws = keep.tile([P, PASSES * H], U8, name="ws", align_bytes=64)
        vq = keep.tile([P, PASSES * H], U32, name="vq", align_bytes=64)
        vs = keep.tile([P, PASSES * H], U8, name="vs", align_bytes=64)
        pq = keep.tile([P, TILES * 256], U32, name="pq", align_bytes=64)
        pscl = keep.tile([P, TILES * 256], U8, name="pscl", align_bytes=64)
        aq = keep.tile([P, TILES * 256], U32, name="aq", align_bytes=64)
        ascl = keep.tile([P, TILES * 256], U8, name="ascl", align_bytes=64)
        bc = const.tile([P, 4 * H], BF16, name="bc")
        gb = const.tile([P, 16], F32, name="gb")
        wz_rows = Wz.rearrange("(a q t) k -> a t q k", q=P, t=4)

        live = {}
        S, V = nc.scalar.copy, nc.vector.tensor_copy

        def load(kind, idx):
            if kind == "a":
                t = rawa.tile([P, H], BF16, tag="rawa")
                src = attention_out[idx * P:(idx + 1) * P, :]
            else:
                t = raw.tile([P, D_IN], BF16, tag="raw")
                if kind == "W":
                    src = wz_rows[idx // 4, idx % 4]
                elif kind == "z":
                    src = z[idx * P:(idx + 1) * P, :]
                else:
                    src = w1_deq[idx * P:(idx + 1) * P, :]
            if kind == "W" and idx == 0:
                for c in (slice(0, D_IN // 2), slice(D_IN // 2, D_IN)):
                    nc.sync.dma_start(out=t[:, c], in_=src[:, c])
            else:
                nc.sync.dma_start(out=t[:], in_=src)
            live[("raw", kind, idx)] = t

        def spread(i):
            nc.sync.dma_start(out=bc[:, i * H:(i + 1) * H], in_=(bz, b1, g1, b1_ln)[i].partition_broadcast(P))

        def tr(kind, idx, b):
            words = live[("raw", kind, idx)][:].bitcast(F32)
            xt = ps_t.tile([P, BANK], F32, tag="tp", name="xt")
            for s in range(4):
                c0 = (2 * b + s // 2) * 256
                nc.tensor.transpose(xt[:, s * P:(s + 1) * P], words[:, c0 + s % 2:c0 + 256:2], ident[:])
            live[("xt", kind, idx, b)] = xt

        def cp(kind, idx, b, eng):
            src = live[("xt", kind, idx, b)][:].rearrange("p (g u r) -> p g r u", g=2, u=2)
            if kind in ("W", "w"):
                key = ("grp", kind, idx // 4)
                if key not in live:
                    live[key] = stagew.tile([P, 4 * D_IN], BF16, tag="grpw", align_bytes=64, name="grpw")
                dst = live[key][:].bitcast(F32).rearrange("p (g j r u) -> p g j r u", g=4, j=4, u=2)[
                    :, 2 * b:2 * b + 2, idx % 4
                ]
            else:
                key = ("grp", kind, idx)
                if key not in live:
                    if kind == "a":
                        live[key] = stage.tile([P, H], BF16, tag="grpa", align_bytes=64, name="grpa")
                    else:
                        live[key] = stage.tile([P, D_IN], BF16, tag="grp", align_bytes=64, name="grp")
                dst = live[key][:].bitcast(F32)[:, b * BANK:(b + 1) * BANK].rearrange("p (g r u) -> p g r u", g=2, u=2)
            eng(out=dst, in_=src)

        def qw(kind, half, g):
            cq, cs = (wq, ws) if kind == "W" else (vq, vs)
            sl = slice(g * H + half * BANK, g * H + (half + 1) * BANK)
            nc.vector.quantize_mx(out=cq[:, sl].bitcast(FP8X4), scales=cs[:, sl], in_=live[("grp", kind, half)][:, g * D_IN:(g + 1) * D_IN])

        def qr(kind, idx):
            words = 512 if kind == "z" else 256
            cq, cs = (zq, zs) if kind == "z" else (aq, ascl)
            sl = slice(idx * words, (idx + 1) * words)
            nc.vector.quantize_mx(out=cq[:, sl].bitcast(FP8X4), scales=cs[:, sl], in_=live[("grp", kind, idx)][:])

        def mx(stg, i, n, first=0, last=4):
            if first == 0:
                live[("acc", stg, i, n)] = ps_a.tile([P, BANK], F32, tag="acc", name="acc")
            acc = live[("acc", stg, i, n)]
            for g in range(first, last):
                if stg == 1:
                    c0 = i * 512 + g * P
                    lq, ls, rq, rs = zq, zs, wq, ws
                else:
                    c0 = i * 256 + (g % 2) * P
                    lq, ls = (pq, pscl) if g < 2 else (aq, ascl)
                    rq, rs = vq, vs
                sl = slice(c0, c0 + P)
                sr = slice(g * H + n * BANK, g * H + (n + 1) * BANK)
                nc.tensor.matmul_mx(out=acc[:], lhsT=lq[:, sl].bitcast(FP8X4), lhsT_scale=ls[:, sl], rhs=rq[:, sr].bitcast(FP8X4), rhs_scale=rs[:, sr], start=(g == 0), stop=(g == PASSES - 1))

        def drain(stg, i, n):
            if n == 0:
                live[("y", stg, i)] = (rows1 if stg == 1 else rows2).tile([P, H], F32, tag="y1" if stg == 1 else "y2", name="y")
                live[("sums", stg, i)] = small.tile([P, 2], F32, tag="sums", name="sums")
            off = (stg - 1) * H + n * BANK
            nc.vector.scalar_tensor_tensor(
                out=live[("y", stg, i)][:, n * BANK:(n + 1) * BANK], in0=live[("acc", stg, i, n)][:], scalar=1.0,
                in1=bc[:, off:off + BANK], op0=ALU.mult, op1=ALU.add, accum_out=live[("sums", stg, i)][:, n:n + 1])

        def nmean_(stg, i):
            junk2 = small.tile([P, 2], F32, tag="junk2")
            live[("nmean", stg, i)] = small.tile([P, 1], F32, tag="nmean", name="nmean")
            nc.scalar.activation(out=junk2[:], in_=live[("sums", stg, i)][:], func=ACT.Identity, scale=-1.0 / H, accum_out=live[("nmean", stg, i)][:])

        def square_(stg, i):
            junk = junkp.tile([P, H], BF16, tag="junk")
            live[("ssq", stg, i)] = small.tile([P, 1], F32, tag="ssq", name="ssq")
            nc.scalar.activation(out=junk[:], in_=live[("y", stg, i)][:], func=ACT.Square, bias=live[("nmean", stg, i)][:], scale=1.0, accum_out=live[("ssq", stg, i)][:])

        def veps_(stg, i):
            live[("veps", stg, i)] = small.tile([P, 1], F32, tag="veps", name="veps")
            nc.scalar.activation(out=live[("veps", stg, i)][:], in_=live[("ssq", stg, i)][:], func=ACT.Identity, scale=1.0 / H, bias=eps[:])

        def pow_(stg, i):
            live[("rstd", stg, i)] = small.tile([P, 1], F32, tag="rstd", name="rstd")
            nc.gpsimd.tensor_tensor(out=live[("rstd", stg, i)][:], in0=live[("veps", stg, i)][:], in1=mhalf[:], op=ALU.pow)

        def norm(i, eng):
            y = live[("y", 1, i)]
            eng(out=y[:], in0=y[:], scalar1=live[("nmean", 1, i)][:], scalar2=live[("rstd", 1, i)][:], op0=ALU.add, op1=ALU.mult)

        def rows_tr(i, g):
            live[("tp", i, g)] = ps_t.tile([P, BANK], F32, tag="tp", name="tp")
            for t in range(4):
                j = 4 * g + t
                nc.tensor.transpose(live[("tp", i, g)][:, t * P:(t + 1) * P], live[("y", 1, i)][:, j * P:(j + 1) * P], ident[:])

        def rows_out(i, g):
            if g == 0:
                live[("planar", i)] = plan.tile([P, H], BF16, tag="planar", name="planar")
            for t in range(4):
                j = 4 * g + t
                nc.scalar.activation(out=live[("planar", i)][:, j * P:(j + 1) * P], in_=live[("tp", i, g)][:, t * P:(t + 1) * P], func=ACT.Identity, scale=gb[:, j:j + 1], bias=gb[:, 8 + j:9 + j])

        def regroup(i):
            live[("gp", i)] = plan.tile([P, H], BF16, tag="gp", align_bytes=64, name="gp")
            (S if i >= TILES - 2 else V)(out=live[("gp", i)][:].rearrange("p (g c t) -> p g c t", g=2, t=4), in_=live[("planar", i)][:].rearrange("p (g t c) -> p g c t", g=2, t=4))

        def quant_p(i):
            sl = slice(i * 256, (i + 1) * 256)
            nc.vector.quantize_mx(out=pq[:, sl].bitcast(FP8X4), scales=pscl[:, sl], in_=live[("gp", i)][:])

        def gain(i):
            live[("t2", i)] = rows3.tile([P, H], F32, tag="t2", name="t2")
            nc.vector.scalar_tensor_tensor(out=live[("t2", i)][:], in0=live[("y", 2, i)][:], scalar=live[("nmean", 2, i)][:], in1=bc[:, 2 * H:3 * H], op0=ALU.add, op1=ALU.mult)

        def parts(i):
            n = 2 if i == TILES - 1 else 1
            return [slice(k * H // n, (k + 1) * H // n) for k in range(n)]

        def shift(i):
            t2 = live[("t2", i)]
            for c in parts(i):
                nc.vector.scalar_tensor_tensor(out=t2[:, c], in0=t2[:, c], scalar=live[("rstd", 2, i)][:], in1=bc[:, 3 * H + c.start:3 * H + c.stop], op0=ALU.mult, op1=ALU.add)

        def gelu(i):
            for c in parts(i):
                nc.scalar.activation(out=live[("t2", i)][:, c], in_=live[("t2", i)][:, c], func=ACT.Gelu)

        def store(i):
            for c in parts(i):
                nc.sync.dma_start(out=out[i * P:(i + 1) * P, c], in_=live[("t2", i)][:, c])

        def bias(half):
            pb = ps_t.tile([P, BANK], F32, tag="tp")
            nc.tensor.matmul(pb[:], lhsT=identb[:, half:half + 1].to_broadcast([P, P]), rhs=vrows1[:], start=True, stop=True)
            nc.vector.tensor_copy(out=bc[:, half * BANK:(half + 1) * BANK].rearrange("p (t q) -> p t q", t=4), in_=pb[:].rearrange("p (q t) -> p t q", t=4))

        def load_gains():
            for w, vec in enumerate((gz, bz_ln)):
                g16 = const.tile([P, 8], BF16, name="g16_%d" % w)
                nc.sync.dma_start(out=g16[:].rearrange("p (a t) -> p a t", a=2), in_=vec.rearrange("(a q t) -> q a t", q=P, t=4))
                live[("g16", w)] = g16

        def gain_columns():
            for w in range(2):
                nc.vector.tensor_copy(out=gb[:, 8 * w:8 * w + 8], in_=live[("g16", w)][:])

        def on(fn, *args):
            if 0 <= args[-1] < TILES:
                fn(*args)

        def words_in(kind, b, i):
            tr(kind, i, b)

        def words_out(kind, b, i):
            cp(kind, i, b, V if kind in ("W", "w") and b and i % 2 else S)

        def words(kind, b, i):
            words_in(kind, b, i)
            words_out(kind, b, i)

        def m1(n, i):
            mx(1, i, n)

        def m2(n, i):
            mx(2, i, n)

        def d1(n, i):
            drain(1, i, n)

        def d2(n, i):
            drain(2, i, n)

        def r_in(g, i):
            rows_tr(i, g)

        def r_out(g, i):
            rows_out(i, g)

        def norm_rows(i):
            norm(i, nc.gpsimd.tensor_scalar)

        for j in range(TILES):
            load("W", j)
            if j == 0:
                nc.sync.dma_start(out=vrows1[0:2, :], in_=bz.rearrange("(a c) -> a c", a=2))
        for r in range(-AHEAD_Z, TILES - AHEAD_A):
            if r + AHEAD_Z < TILES:
                load("z", r + AHEAD_Z)
            for j in (2 * (r + AHEAD_Z), 2 * (r + AHEAD_Z) + 1):
                if j < TILES:
                    load("w", j)
                if j % 2 == 0 and r + AHEAD_A >= 0:
                    load("a", r + AHEAD_A)
            if r == -2:
                load_gains()
            if -2 <= r <= 0:
                spread(r + 3)
        for j in range(TILES):
            words("W", 0, j)
            words("W", 1, j)
            if j == 0:
                bias(0)
                bias(1)
            if j == 4:
                for g in range(PASSES):
                    qw("W", 0, g)

        for r in range(-AHEAD_Z, TILES + DRAIN_ROUNDS):
            u = 2 * (r + AHEAD_Z)
            if r == -AHEAD_ROWS:
                gain_columns()
            on(words, "z", 0, r + 5)
            on(m2, 0, r)
            on(veps_, 2, r - 1)
            on(gain, r - 1)
            on(words, "z", 1, r + 5)
            on(pow_, 2, r - 1)
            on(d2, 0, r)
            if u == 0:
                for g in range(PASSES):
                    qw("W", 1, g)
            elif u in (4, 8):
                for g in range(PASSES):
                    qw("w", u // 4 - 1, g)
            on(qr, "a", r + 2)
            on(words, "w", 1, u)
            on(square_, 1, r + 3)
            on(words, "a", 0, r + 3)
            on(words, "w", 0, u)
            on(veps_, 1, r + 3)
            on(regroup, r + 1)
            on(gelu, r - 2)
            on(m2, 1, r)
            on(pow_, 1, r + 3)
            on(store, r - 3)
            on(d2, 1, r)
            on(quant_p, r + 1)
            on(m1, 0, r + 4)
            on(qr, "z", r + 5)
            on(nmean_, 2, r)
            on(r_in, 0, r + 2)
            on(words, "w", 0, u + 1)
            on(r_out, 0, r + 2)
            on(words, "w", 1, u + 1)
            on(m1, 1, r + 4)
            on(norm_rows, r + 3)
            on(r_in, 1, r + 2)
            on(square_, 2, r)
            on(d1, 0, r + 4)
            on(d1, 1, r + 4)
            on(nmean_, 1, r + 4)
            on(r_out, 1, r + 2)
            on(shift, r - 1)
